import numpy as np
import ml_dtypes


def mxq(x, axis, fmt="e4m3"):
    dtype, down = {"e4m3": (ml_dtypes.float8_e4m3fn, 7), "e5m2": (ml_dtypes.float8_e5m2, 14)}[fmt]
    v = np.moveaxis(np.asarray(x, np.float32).astype(ml_dtypes.bfloat16).astype(np.float64), axis, -1)
    blocks = v.reshape(v.shape[:-1] + (-1, 32))
    amax = np.abs(blocks).max(-1, keepdims=True)
    byte = np.maximum(np.where(amax > 0, np.frexp(amax)[1] - 1 + 127, 0) - down, 1)
    scale = np.exp2(byte - 127.0)
    codes = (blocks / scale).astype(np.float32).astype(dtype).astype(np.float64)
    return np.moveaxis((codes * scale).reshape(v.shape), -1, axis)


WIDE = False


def mx_kscale(k):
    if not WIDE:
        return np.ones(k)
    levels = np.array([10, -10, 5, -5, 0])
    a = np.random.permutation(np.resize(levels, k // 512 * 4)).reshape(k // 512, 4)
    idx = np.arange(k)
    return np.exp2(a[idx // 512, idx % 128 // 32])


BF16 = ml_dtypes.bfloat16


def bf(x):
    return np.asarray(x, np.float32).astype(BF16)


def f64(x):
    return np.asarray(x).astype(np.float64)


E2M1 = np.array([0.0, 0.5, 1.0, 1.5, 2.0, 3.0, 4.0, 6.0, -0.0, -0.5, -1.0, -1.5, -2.0, -3.0, -4.0, -6.0])


def pack_weight(w, fmt):
    k, n = w.shape
    w = f64(bf(w)).reshape(k // 32, 32, n)
    amax = np.abs(w).max(1)
    if fmt == "e4m3":
        byte = np.frexp(amax)[1] - 1 + 127 - 7
    else:
        mant, ex = np.frexp(amax / 6.0)
        byte = np.where(mant > 0.5, ex, ex - 1) + 127
    byte = np.clip(np.where(amax > 0, byte, 1), 1, 254)
    scaled = (w * np.exp2(127.0 - byte)[:, None, :]).reshape(k, n).astype(np.float32)
    by_word = np.ascontiguousarray(scaled.reshape(k // 512, 128, 4, n).transpose(0, 1, 3, 2))
    if fmt == "e4m3":
        words = by_word.astype(ml_dtypes.float8_e4m3fn).view(np.uint8)
    else:
        c = by_word.astype(ml_dtypes.float4_e2m1fn).view(np.uint8) & 0xF
        words = c[..., 0::2] | (c[..., 1::2] << 4)
    return np.ascontiguousarray(words), np.ascontiguousarray(byte.astype(np.uint8).reshape(k // 512, 16, n))


def unpack_weight(words, scales, fmt):
    g, p, n, _ = words.shape
    if fmt == "e4m3":
        vals = np.ascontiguousarray(words).view(ml_dtypes.float8_e4m3fn).astype(np.float64)
    else:
        nib = np.empty((g, p, n, 4), np.uint8)
        nib[..., 0::2] = words & 0xF
        nib[..., 1::2] = words >> 4
        vals = E2M1[nib]
    vals = vals * np.repeat(np.exp2(scales.astype(np.float64) - 127.0), 8, axis=1)[..., None]
    return vals.transpose(0, 1, 3, 2).reshape(g * 512, n)


N, IN_DIM, HID, OUT_DIM = 4096, 512, 128, 256


def setup_inputs():
    s = mx_kscale(IN_DIM)
    X = bf(np.random.standard_normal((N, IN_DIM)) * s)
    A = bf(np.random.uniform(0.0, 1.0, (N, N)) * 0.5 / np.sqrt(N))
    W_in_words, W_in_scales = pack_weight(np.random.standard_normal((IN_DIM, HID)) / np.sqrt(IN_DIM) / s[:, None], "e4m3")
    b_in = bf(np.random.standard_normal(HID) * 0.1)
    eps0 = bf(np.random.uniform(0.2, 0.4, (1,)))
    return {"X": X,
            "A": A,
            "W_in_words": W_in_words,
            "W_in_scales": W_in_scales,
            "b_in": b_in,
            "eps0": eps0}


def reference(X, A, W_in_words, W_in_scales, b_in, eps0):
    h = (mxq(f64(X), 1, "e4m3") @ unpack_weight(W_in_words, W_in_scales, "e4m3")) + f64(b_in)
    return (mxq(f64(A), 1, "e4m3") @ mxq(h, 0, "e4m3")) + (1.0 + f64(eps0)) * h

@@ -1,0 +1,227 @@
+from contextlib import ExitStack
+
+import concourse.masks as masks
+import concourse.mybir as mybir
+
+F32 = mybir.dt.float32
+BF16 = mybir.dt.bfloat16
+I32 = mybir.dt.int32
+U32 = mybir.dt.uint32
+U8 = mybir.dt.uint8
+FP8X4 = mybir.dt.float8_e4m3fn_x4
+ADD = mybir.AluOpType.add
+MULT = mybir.AluOpType.mult
+
+P = 128
+PACK = 4
+K_PASS = P * PACK
+NODES = 4096
+IN_DIM = 512
+HID = 128
+GROUPS = NODES // K_PASS
+
+OPERANDS = 8
+BANKS_PER_UNIT = 4
+X_LOADS = 4
+A_LOADS = 16
+A_BUFS = 6
+
+FLOPS = 2 * NODES * IN_DIM * HID + 2 * NODES * NODES * HID
+
+
+def tile_gin_pa_t_kernel(tc, X, A, W_in_words, W_in_scales, b_in, eps0, out):
+    nc = tc.nc
+
+    x_view = X.rearrange("(x q p e) k -> x p q (e k)", x=X_LOADS, q=4, p=P, e=2)
+    a_view = A.rearrange("(d p e) k -> d p (e k)", d=A_LOADS, p=P, e=2)
+    out_view = out.rearrange("(g u p e) n -> g p u (e n)", g=GROUPS, u=2, p=P, e=2)
+
+    with ExitStack() as ctx:
+        const = ctx.enter_context(tc.tile_pool(name="const", bufs=1))
+        x_pool = ctx.enter_context(tc.tile_pool(name="x_rows", bufs=X_LOADS))
+        a_pool = ctx.enter_context(tc.tile_pool(name="a_rows", bufs=A_BUFS))
+        grouped_pool = ctx.enter_context(tc.tile_pool(name="grouped", bufs=4))
+        mx_pool = ctx.enter_context(tc.tile_pool(name="mx", bufs=4))
+        out_pool = ctx.enter_context(tc.tile_pool(name="result", bufs=2))
+        transposed_banks = ctx.enter_context(tc.psum_pool(name="transposed", bufs=6))
+        sum_banks = ctx.enter_context(tc.psum_pool(name="sums", bufs=2))
+        ctx.enter_context(tc.manual_schedule())
+
+        ident = const.tile([P, P], F32, name="ident")
+        masks.make_identity(nc, ident[:])
+
+        w_scales = const.tile([P, HID], U8, name="w_scales", align_bytes=64)
+        nc.vector.memset(w_scales[:].bitcast(I32), 0)
+        for quadrant in range(4):
+            nc.sync.dma_start(
+                out=w_scales[32 * quadrant : 32 * quadrant + 4, :].bitcast(I32),
+                in_=W_in_scales[0, 4 * quadrant : 4 * quadrant + 4, :].bitcast(I32),
+            )
+        w_codes = const.tile([P, HID * PACK], U8, name="w_codes", align_bytes=64)
+        nc.sync.dma_start(
+            out=w_codes[:].bitcast(I32),
+            in_=W_in_words[0].rearrange("p n t -> p (n t)").bitcast(I32),
+        )
+
+        bias_bf = const.tile([P, HID], BF16, name="bias_bf")
+        nc.scalar.dma_start(out=bias_bf[:], in_=b_in.partition_broadcast(P))
+        eps_bf = const.tile([P, 1], BF16, name="eps_bf")
+        nc.scalar.dma_start(out=eps_bf[:], in_=eps0.partition_broadcast(P))
+
+        x_rows = []
+        for x in range(X_LOADS):
+            rows = x_pool.tile([P, OPERANDS, IN_DIM], BF16, name="x_rows")
+            nc.sync.dma_start(
+                out=rows[:].rearrange("p (q e) k -> p q (e k)", e=2), in_=x_view[x]
+            )
+            x_rows.append(rows)
+
+        a_rows = {}
+
+        def load_a(d):
+            rows = a_pool.tile([P, 2, NODES], BF16, name="a_rows")
+            nc.sync.dma_start(out=rows[:].rearrange("p e k -> p (e k)"), in_=a_view[d])
+            a_rows[d] = rows
+
+        for d in range(A_BUFS):
+            load_a(d)
+
+        bias = const.tile([P, HID], F32, name="bias")
+        nc.vector.tensor_copy(out=bias[:], in_=bias_bf[:])
+        self_weight = const.tile([P, 1], F32, name="self_weight")
+        nc.vector.tensor_scalar_add(out=self_weight[:], in0=eps_bf[:], scalar1=1.0)
+        bias_self = const.tile([P, HID], F32, name="bias_self")
+        nc.vector.tensor_scalar_mul(out=bias_self[:], in0=bias[:], scalar1=self_weight[:, 0:1])
+
+        h_grouped = const.tile([P, GROUPS, HID, PACK], BF16, name="h_grouped", align_bytes=64)
+        h_codes = const.tile([P, GROUPS * HID], U32, name="h_codes", align_bytes=64)
+        h_scales = const.tile([P, GROUPS * HID], U8, name="h_scales", align_bytes=64)
+        h_self = const.tile([P, GROUPS, PACK, HID], F32, name="h_self")
+
+        def transpose_and_group(word_block, vector_banks):
+            grouped = grouped_pool.tile(
+                [P, OPERANDS, P, PACK], BF16, name="grouped", align_bytes=64
+            )
+            grouped_words = grouped[:].bitcast(F32)
+            for b in range(BANKS_PER_UNIT):
+                bank = transposed_banks.tile([P, 2, 2, P], F32, name="bank")
+                for j in range(2):
+                    for v in range(2):
+                        nc.tensor.transpose(bank[:, j, v, :], word_block(2 * b + j, v), ident[:])
+                planes_alternately = bank[:].rearrange("p j v r -> p j r v")
+                target = grouped_words[:, 2 * b : 2 * b + 2, :, :]
+                if b < vector_banks:
+                    nc.vector.tensor_copy(out=target, in_=planes_alternately)
+                else:
+                    nc.scalar.copy(out=target, in_=planes_alternately)
+            return grouped
+
+        def quantise(grouped):
+            codes = mx_pool.tile([P, OPERANDS * P], U32, name="codes", align_bytes=64)
+            scales = mx_pool.tile([P, OPERANDS * P], U8, name="scales", align_bytes=64)
+            nc.vector.quantize_mx(
+                out=codes[:].bitcast(FP8X4),
+                scales=scales[:],
+                in_=grouped[:].rearrange("p i r t -> p (i r t)"),
+            )
+            return codes, scales
+
+        def project(x, codes, scales):
+            h_sums = []
+            for half in range(2):
+                h_sum = sum_banks.tile([P, PACK, HID], F32, name="h_sum", tag="sums")
+                for t in range(PACK):
+                    cols = slice((PACK * half + t) * P, (PACK * half + t + 1) * P)
+                    nc.tensor.matmul_mx(
+                        out=h_sum[:, t, :],
+                        lhsT=codes[:, cols].bitcast(FP8X4),
+                        lhsT_scale=scales[:, cols],
+                        rhs=w_codes[:].bitcast(FP8X4),
+                        rhs_scale=w_scales[:],
+                        start=True,
+                        stop=True,
+                    )
+                h_sums.append(h_sum)
+            for half in range(2):
+                nc.vector.tensor_tensor(
+                    out=h_grouped[:, 2 * x + half],
+                    in0=h_sums[half][:].rearrange("p t n -> p n t"),
+                    in1=bias[:].unsqueeze(2).to_broadcast([P, HID, PACK]),
+                    op=ADD,
+                )
+
+            def keep_self_term(half):
+                nc.vector.scalar_tensor_tensor(
+                    out=h_self[:, 2 * x + half],
+                    in0=h_sums[half][:],
+                    scalar=self_weight[:, 0:1],
+                    in1=bias_self[:].unsqueeze(1).to_broadcast([P, PACK, HID]),
+                    op0=MULT,
+                    op1=ADD,
+                )
+
+            keep_self_term(0)
+            cols = slice(2 * x * HID, (2 * x + 2) * HID)
+            nc.vector.quantize_mx(
+                out=h_codes[:, cols].bitcast(FP8X4),
+                scales=h_scales[:, cols],
+                in_=h_grouped[:, 2 * x : 2 * x + 2].rearrange("p g n t -> p (g n t)"),
+            )
+            keep_self_term(1)
+
+        out_sums = {}
+
+        def aggregate(r, codes, scales):
+            g, t = divmod(r, PACK)
+            if t == 0:
+                out_sums[g] = sum_banks.tile([P, PACK, HID], F32, name="out_sum", tag="sums")
+            for c in range(GROUPS):
+                cols = slice(c * P, (c + 1) * P)
+                nc.tensor.matmul_mx(
+                    out=out_sums[g][:, t, :],
+                    lhsT=codes[:, cols].bitcast(FP8X4),
+                    lhsT_scale=scales[:, cols],
+                    rhs=h_codes[:, cols].bitcast(FP8X4),
+                    rhs_scale=h_scales[:, cols],
+                    start=(c == 0),
+                    stop=(c == GROUPS - 1),
+                )
+            if t == PACK - 1:
+                result = out_pool.tile([P, PACK, HID], F32, name="result")
+                nc.vector.tensor_tensor(
+                    out=result[:], in0=out_sums[g][:], in1=h_self[:, g], op=ADD
+                )
+                nc.sync.dma_start(
+                    out=out_view[g], in_=result[:].rearrange("p (u e) n -> p u (e n)", e=2)
+                )
+
+        def x_word_block(x):
+            words = x_rows[x][:].bitcast(F32)
+            return lambda i, v: words[:, i, v : IN_DIM // 2 : 2]
+
+        def a_word_block(d, e):
+            words = a_rows[d][:].bitcast(F32)
+            return lambda c, v: words[:, e, (2 * c + v) * P : (2 * c + v + 1) * P]
+
+        before = None
+        for x in range(X_LOADS):
+            quantised = quantise(transpose_and_group(x_word_block(x), vector_banks=0))
+            if x > 0:
+                project(x - 1, before[0], before[1])
+            before = quantised
+
+        for d in range(A_LOADS):
+            grouped_tiles = [
+                transpose_and_group(a_word_block(d, e), vector_banks=1) for e in range(2)
+            ]
+            if d + A_BUFS < A_LOADS:
+                load_a(d + A_BUFS)
+            quantised = [quantise(grouped) for grouped in grouped_tiles]
+            if d == 0:
+                project(X_LOADS - 1, before[0], before[1])
+            else:
+                for e in range(2):
+                    aggregate(2 * (d - 1) + e, before[e][0], before[e][1])
+            before = quantised
+        for e in range(2):
+            aggregate(2 * (A_LOADS - 1) + e, before[e][0], before[e][1])

@@ -18,13 +18,11 @@ K_PASS = P * PACK
 NODES = 4096
 IN_DIM = 512
 HID = 128
-GROUPS = NODES // K_PASS
-
-OPERANDS = 8
-BANKS_PER_UNIT = 4
-X_LOADS = 4
-A_LOADS = 16
-A_BUFS = 6
+NODE_TILES = NODES // P
+PASSES = NODES // K_PASS
+A_LOADS = NODE_TILES // 2
+A_BUFS = 5
+ROW_TILES_PER_ROUND = 1
 
 FLOPS = 2 * NODES * IN_DIM * HID + 2 * NODES * NODES * HID
 
@@ -32,23 +30,36 @@ FLOPS = 2 * NODES * IN_DIM * HID + 2 * NODES * NODES * HID
 def tile_gin_pa_t_kernel(tc, X, A, W_in_words, W_in_scales, b_in, eps0, out):
     nc = tc.nc
 
-    x_view = X.rearrange("(x q p e) k -> x p q (e k)", x=X_LOADS, q=4, p=P, e=2)
+    x_view = X.rearrange("(g q p e) k -> g p q (e k)", g=PASSES, q=2, p=P, e=2)
     a_view = A.rearrange("(d p e) k -> d p (e k)", d=A_LOADS, p=P, e=2)
-    out_view = out.rearrange("(g u p e) n -> g p u (e n)", g=GROUPS, u=2, p=P, e=2)
+    out_view = out.rearrange("(d p e) n -> d p (e n)", d=A_LOADS, p=P, e=2)
 
     with ExitStack() as ctx:
         const = ctx.enter_context(tc.tile_pool(name="const", bufs=1))
-        x_pool = ctx.enter_context(tc.tile_pool(name="x_rows", bufs=X_LOADS))
+        x_pool = ctx.enter_context(tc.tile_pool(name="x_rows", bufs=PASSES))
         a_pool = ctx.enter_context(tc.tile_pool(name="a_rows", bufs=A_BUFS))
-        grouped_pool = ctx.enter_context(tc.tile_pool(name="grouped", bufs=4))
-        mx_pool = ctx.enter_context(tc.tile_pool(name="mx", bufs=4))
-        out_pool = ctx.enter_context(tc.tile_pool(name="result", bufs=2))
+        grouped_pool = ctx.enter_context(
+            tc.tile_pool(name="grouped", bufs=2 * ROW_TILES_PER_ROUND + 1)
+        )
+        mx_pool = ctx.enter_context(tc.tile_pool(name="mx", bufs=2 * ROW_TILES_PER_ROUND + 1))
+        result_pool = ctx.enter_context(tc.tile_pool(name="result", bufs=A_LOADS))
         transposed_banks = ctx.enter_context(tc.psum_pool(name="transposed", bufs=6))
         sum_banks = ctx.enter_context(tc.psum_pool(name="sums", bufs=2))
         ctx.enter_context(tc.manual_schedule())
 
         ident = const.tile([P, P], F32, name="ident")
         masks.make_identity(nc, ident[:])
+
+        x_rows = []
+
+        def load_x(g):
+            rows = x_pool.tile([P, PACK, IN_DIM], BF16, name="x_rows")
+            nc.sync.dma_start(
+                out=rows[:].rearrange("p (q e) k -> p q (e k)", e=2), in_=x_view[g]
+            )
+            x_rows.append(rows)
+
+        load_x(0)
 
         w_scales = const.tile([P, HID], U8, name="w_scales", align_bytes=64)
         nc.vector.memset(w_scales[:].bitcast(I32), 0)
@@ -62,48 +73,42 @@ def tile_gin_pa_t_kernel(tc, X, A, W_in_words, W_in_scales, b_in, eps0, out):
             out=w_codes[:].bitcast(I32),
             in_=W_in_words[0].rearrange("p n t -> p (n t)").bitcast(I32),
         )
-
         bias_bf = const.tile([P, HID], BF16, name="bias_bf")
         nc.scalar.dma_start(out=bias_bf[:], in_=b_in.partition_broadcast(P))
         eps_bf = const.tile([P, 1], BF16, name="eps_bf")
         nc.scalar.dma_start(out=eps_bf[:], in_=eps0.partition_broadcast(P))
 
-        x_rows = []
-        for x in range(X_LOADS):
-            rows = x_pool.tile([P, OPERANDS, IN_DIM], BF16, name="x_rows")
-            nc.sync.dma_start(
-                out=rows[:].rearrange("p (q e) k -> p q (e k)", e=2), in_=x_view[x]
-            )
-            x_rows.append(rows)
+        for g in range(1, PASSES):
+            load_x(g)
 
-        a_rows = {}
+        a_rows = []
 
-        def load_a(d):
+        def load_a():
             rows = a_pool.tile([P, 2, NODES], BF16, name="a_rows")
-            nc.sync.dma_start(out=rows[:].rearrange("p e k -> p (e k)"), in_=a_view[d])
-            a_rows[d] = rows
+            nc.sync.dma_start(
+                out=rows[:].rearrange("p e k -> p (e k)"), in_=a_view[len(a_rows)]
+            )
+            a_rows.append(rows)
 
         for d in range(A_BUFS):
-            load_a(d)
+            load_a()
 
         bias = const.tile([P, HID], F32, name="bias")
         nc.vector.tensor_copy(out=bias[:], in_=bias_bf[:])
         self_weight = const.tile([P, 1], F32, name="self_weight")
         nc.vector.tensor_scalar_add(out=self_weight[:], in0=eps_bf[:], scalar1=1.0)
-        bias_self = const.tile([P, HID], F32, name="bias_self")
-        nc.vector.tensor_scalar_mul(out=bias_self[:], in0=bias[:], scalar1=self_weight[:, 0:1])
 
-        h_grouped = const.tile([P, GROUPS, HID, PACK], BF16, name="h_grouped", align_bytes=64)
-        h_codes = const.tile([P, GROUPS * HID], U32, name="h_codes", align_bytes=64)
-        h_scales = const.tile([P, GROUPS * HID], U8, name="h_scales", align_bytes=64)
-        h_self = const.tile([P, GROUPS, PACK, HID], F32, name="h_self")
+        h_f32 = const.tile([P, NODE_TILES, HID], F32, name="h_f32")
+        h_grouped = const.tile([P, PASSES, HID, PACK], BF16, name="h_grouped", align_bytes=64)
+        h_codes = const.tile([P, PASSES * HID], U32, name="h_codes", align_bytes=64)
+        h_scales = const.tile([P, PASSES * HID], U8, name="h_scales", align_bytes=64)
 
-        def transpose_and_group(word_block, vector_banks):
+        def transpose_and_group(word_block, operands, vector_banks):
             grouped = grouped_pool.tile(
-                [P, OPERANDS, P, PACK], BF16, name="grouped", align_bytes=64
+                [P, operands, P, PACK], BF16, name="grouped", align_bytes=64
             )
             grouped_words = grouped[:].bitcast(F32)
-            for b in range(BANKS_PER_UNIT):
+            for b in range(operands // 2):
                 bank = transposed_banks.tile([P, 2, 2, P], F32, name="bank")
                 for j in range(2):
                     for v in range(2):
@@ -116,9 +121,9 @@ def tile_gin_pa_t_kernel(tc, X, A, W_in_words, W_in_scales, b_in, eps0, out):
                     nc.scalar.copy(out=target, in_=planes_alternately)
             return grouped
 
-        def quantise(grouped):
-            codes = mx_pool.tile([P, OPERANDS * P], U32, name="codes", align_bytes=64)
-            scales = mx_pool.tile([P, OPERANDS * P], U8, name="scales", align_bytes=64)
+        def quantise(grouped, operands):
+            codes = mx_pool.tile([P, operands * P], U32, name="codes", align_bytes=64)
+            scales = mx_pool.tile([P, operands * P], U8, name="scales", align_bytes=64)
             nc.vector.quantize_mx(
                 out=codes[:].bitcast(FP8X4),
                 scales=scales[:],
@@ -126,102 +131,113 @@ def tile_gin_pa_t_kernel(tc, X, A, W_in_words, W_in_scales, b_in, eps0, out):
             )
             return codes, scales
 
-        def project(x, codes, scales):
-            h_sums = []
-            for half in range(2):
-                h_sum = sum_banks.tile([P, PACK, HID], F32, name="h_sum", tag="sums")
-                for t in range(PACK):
-                    cols = slice((PACK * half + t) * P, (PACK * half + t + 1) * P)
-                    nc.tensor.matmul_mx(
-                        out=h_sum[:, t, :],
-                        lhsT=codes[:, cols].bitcast(FP8X4),
-                        lhsT_scale=scales[:, cols],
-                        rhs=w_codes[:].bitcast(FP8X4),
-                        rhs_scale=w_scales[:],
-                        start=True,
-                        stop=True,
-                    )
-                h_sums.append(h_sum)
-            for half in range(2):
-                nc.vector.tensor_tensor(
-                    out=h_grouped[:, 2 * x + half],
-                    in0=h_sums[half][:].rearrange("p t n -> p n t"),
-                    in1=bias[:].unsqueeze(2).to_broadcast([P, HID, PACK]),
-                    op=ADD,
-                )
+        def x_word_block(g):
+            words = x_rows[g][:].bitcast(F32)
+            return lambda t, v: words[:, t, v : IN_DIM // 2 : 2]
 
-            def keep_self_term(half):
-                nc.vector.scalar_tensor_tensor(
-                    out=h_self[:, 2 * x + half],
-                    in0=h_sums[half][:],
-                    scalar=self_weight[:, 0:1],
-                    in1=bias_self[:].unsqueeze(1).to_broadcast([P, PACK, HID]),
-                    op0=MULT,
-                    op1=ADD,
+        def project(g, codes, scales):
+            h_sum = sum_banks.tile([P, PACK, HID], F32, name="h_sum", tag="sums")
+            for t in range(PACK):
+                cols = slice(t * P, (t + 1) * P)
+                nc.tensor.matmul_mx(
+                    out=h_sum[:, t, :],
+                    lhsT=codes[:, cols].bitcast(FP8X4),
+                    lhsT_scale=scales[:, cols],
+                    rhs=w_codes[:].bitcast(FP8X4),
+                    rhs_scale=w_scales[:],
+                    start=True,
+                    stop=True,
                 )
+            h_tiles = h_f32[:, PACK * g : PACK * (g + 1), :]
+            nc.vector.tensor_tensor(
+                out=h_tiles,
+                in0=h_sum[:],
+                in1=bias[:].unsqueeze(1).to_broadcast([P, PACK, HID]),
+                op=ADD,
+            )
+            nc.scalar.copy(out=h_grouped[:, g], in_=h_tiles.rearrange("p t n -> p n t"))
 
-            keep_self_term(0)
-            cols = slice(2 * x * HID, (2 * x + 2) * HID)
+        def quantise_h(g):
+            cols = slice(g * HID, (g + 1) * HID)
             nc.vector.quantize_mx(
                 out=h_codes[:, cols].bitcast(FP8X4),
                 scales=h_scales[:, cols],
-                in_=h_grouped[:, 2 * x : 2 * x + 2].rearrange("p g n t -> p (g n t)"),
+                in_=h_grouped[:, g].rearrange("p n t -> p (n t)"),
             )
-            keep_self_term(1)
+
+        x_grouped = {}
+        x_mx = {}
+        for turn in range(PASSES + 3):
+            if turn < PASSES:
+                x_grouped[turn] = transpose_and_group(x_word_block(turn), PACK, vector_banks=0)
+            if 0 <= turn - 1 < PASSES:
+                x_mx[turn - 1] = quantise(x_grouped[turn - 1], PACK)
+            if 0 <= turn - 2 < PASSES:
+                project(turn - 2, x_mx[turn - 2][0], x_mx[turn - 2][1])
+            if 0 <= turn - 3 < PASSES:
+                quantise_h(turn - 3)
+
+        def a_word_block(r):
+            words = a_rows[r // 2][:].bitcast(F32)
+            return lambda c, v: words[:, r % 2, (2 * c + v) * P : (2 * c + v + 1) * P]
 
         out_sums = {}
+        results = {}
+
+        def store(d):
+            nc.sync.dma_start(out=out_view[d], in_=results[d][:].rearrange("p e n -> p (e n)"))
 
         def aggregate(r, codes, scales):
-            g, t = divmod(r, PACK)
-            if t == 0:
-                out_sums[g] = sum_banks.tile([P, PACK, HID], F32, name="out_sum", tag="sums")
-            for c in range(GROUPS):
+            d, e = divmod(r, 2)
+            if e == 0:
+                out_sums[d] = sum_banks.tile([P, 2, HID], F32, name="out_sum", tag="sums")
+            for c in range(PASSES):
                 cols = slice(c * P, (c + 1) * P)
                 nc.tensor.matmul_mx(
-                    out=out_sums[g][:, t, :],
+                    out=out_sums[d][:, e, :],
                     lhsT=codes[:, cols].bitcast(FP8X4),
                     lhsT_scale=scales[:, cols],
                     rhs=h_codes[:, cols].bitcast(FP8X4),
                     rhs_scale=h_scales[:, cols],
                     start=(c == 0),
-                    stop=(c == GROUPS - 1),
+                    stop=(c == PASSES - 1),
                 )
-            if t == PACK - 1:
-                result = out_pool.tile([P, PACK, HID], F32, name="result")
-                nc.vector.tensor_tensor(
-                    out=result[:], in0=out_sums[g][:], in1=h_self[:, g], op=ADD
+            if e == 1:
+                results[d] = result_pool.tile([P, 2, HID], F32, name="result")
+                nc.vector.scalar_tensor_tensor(
+                    out=results[d][:],
+                    in0=h_f32[:, 2 * d : 2 * d + 2, :],
+                    scalar=self_weight[:, 0:1],
+                    in1=out_sums[d][:],
+                    op0=MULT,
+                    op1=ADD,
                 )
-                nc.sync.dma_start(
-                    out=out_view[g], in_=result[:].rearrange("p (u e) n -> p u (e n)", e=2)
-                )
+                if len(a_rows) == A_LOADS:
+                    store(d)
 
-        def x_word_block(x):
-            words = x_rows[x][:].bitcast(F32)
-            return lambda i, v: words[:, i, v : IN_DIM // 2 : 2]
+        def load_next_a():
+            if len(a_rows) < A_LOADS:
+                load_a()
+                if len(a_rows) == A_LOADS:
+                    for d in sorted(results):
+                        store(d)
 
-        def a_word_block(d, e):
-            words = a_rows[d][:].bitcast(F32)
-            return lambda c, v: words[:, e, (2 * c + v) * P : (2 * c + v + 1) * P]
+        rounds = NODE_TILES // ROW_TILES_PER_ROUND
 
-        before = None
-        for x in range(X_LOADS):
-            quantised = quantise(transpose_and_group(x_word_block(x), vector_banks=0))
-            if x > 0:
-                project(x - 1, before[0], before[1])
-            before = quantised
+        def row_tiles(turn):
+            return range(turn * ROW_TILES_PER_ROUND, (turn + 1) * ROW_TILES_PER_ROUND)
 
-        for d in range(A_LOADS):
-            grouped_tiles = [
-                transpose_and_group(a_word_block(d, e), vector_banks=1) for e in range(2)
-            ]
-            if d + A_BUFS < A_LOADS:
-                load_a(d + A_BUFS)
-            quantised = [quantise(grouped) for grouped in grouped_tiles]
-            if d == 0:
-                project(X_LOADS - 1, before[0], before[1])
-            else:
-                for e in range(2):
-                    aggregate(2 * (d - 1) + e, before[e][0], before[e][1])
-            before = quantised
-        for e in range(2):
-            aggregate(2 * (A_LOADS - 1) + e, before[e][0], before[e][1])
+        a_grouped = {}
+        a_mx = {}
+        for turn in range(rounds + 2):
+            if turn < rounds:
+                for r in row_tiles(turn):
+                    a_grouped[r] = transpose_and_group(a_word_block(r), PASSES, vector_banks=1)
+                    if r % 2 == 1:
+                        load_next_a()
+            if 0 <= turn - 1 < rounds:
+                for r in row_tiles(turn - 1):
+                    a_mx[r] = quantise(a_grouped[r], PASSES)
+            if 0 <= turn - 2 < rounds:
+                for r in row_tiles(turn - 2):
+                    aggregate(r, a_mx[r][0], a_mx[r][1])

@@ -73,10 +73,10 @@ def tile_gin_pa_t_kernel(tc, X, A, W_in_words, W_in_scales, b_in, eps0, out):
             out=w_codes[:].bitcast(I32),
             in_=W_in_words[0].rearrange("p n t -> p (n t)").bitcast(I32),
         )
-        bias_bf = const.tile([P, HID], BF16, name="bias_bf")
-        nc.scalar.dma_start(out=bias_bf[:], in_=b_in.partition_broadcast(P))
-        eps_bf = const.tile([P, 1], BF16, name="eps_bf")
-        nc.scalar.dma_start(out=eps_bf[:], in_=eps0.partition_broadcast(P))
+        small_rows = const.tile([P, 2 * HID], BF16, name="small_rows")
+        nc.vector.memset(small_rows[:], 0.0)
+        nc.scalar.dma_start(out=small_rows[0:1, 0:HID], in_=b_in.unsqueeze(0))
+        nc.scalar.dma_start(out=small_rows[0:1, HID : HID + 1], in_=eps0.unsqueeze(0))
 
         for g in range(1, PASSES):
             load_x(g)
@@ -93,10 +93,16 @@ def tile_gin_pa_t_kernel(tc, X, A, W_in_words, W_in_scales, b_in, eps0, out):
         for d in range(A_BUFS):
             load_a()
 
+        ones = const.tile([P, P], BF16, name="ones")
+        nc.vector.memset(ones[:], 1.0)
+        spread = sum_banks.tile([P, 2 * HID], F32, name="spread", tag="sums")
+        nc.tensor.matmul(out=spread[:], lhsT=ones[:], rhs=small_rows[:], start=True, stop=True)
         bias = const.tile([P, HID], F32, name="bias")
-        nc.vector.tensor_copy(out=bias[:], in_=bias_bf[:])
+        nc.vector.tensor_copy(out=bias[:], in_=spread[:, 0:HID])
         self_weight = const.tile([P, 1], F32, name="self_weight")
-        nc.vector.tensor_scalar_add(out=self_weight[:], in0=eps_bf[:], scalar1=1.0)
+        nc.vector.tensor_scalar_add(
+            out=self_weight[:], in0=spread[:, HID : HID + 1], scalar1=1.0
+        )
 
         h_f32 = const.tile([P, NODE_TILES, HID], F32, name="h_f32")
         h_grouped = const.tile([P, PASSES, HID, PACK], BF16, name="h_grouped", align_bytes=64)

@@ -175,7 +175,7 @@ def tile_gin_pa_t_kernel(tc, X, A, W_in_words, W_in_scales, b_in, eps0, out):
         x_mx = {}
         for turn in range(PASSES + 3):
             if turn < PASSES:
-                x_grouped[turn] = transpose_and_group(x_word_block(turn), PACK, vector_banks=0)
+                x_grouped[turn] = transpose_and_group(x_word_block(turn), PACK, vector_banks=1)
             if 0 <= turn - 1 < PASSES:
                 x_mx[turn - 1] = quantise(x_grouped[turn - 1], PACK)
             if 0 <= turn - 2 < PASSES:
@@ -238,7 +238,9 @@ def tile_gin_pa_t_kernel(tc, X, A, W_in_words, W_in_scales, b_in, eps0, out):
         for turn in range(rounds + 2):
             if turn < rounds:
                 for r in row_tiles(turn):
-                    a_grouped[r] = transpose_and_group(a_word_block(r), PASSES, vector_banks=1)
+                    a_grouped[r] = transpose_and_group(
+                        a_word_block(r), PASSES, vector_banks=r % 2
+                    )
                     if r % 2 == 1:
                         load_next_a()
             if 0 <= turn - 1 < rounds:

@@ -22,7 +22,7 @@ NODE_TILES = NODES // P
 PASSES = NODES // K_PASS
 A_LOADS = NODE_TILES // 2
 A_BUFS = 5
-ROW_TILES_PER_ROUND = 1
+STORE_TILES = 4
 
 FLOPS = 2 * NODES * IN_DIM * HID + 2 * NODES * NODES * HID
 
@@ -31,18 +31,17 @@ def tile_gin_pa_t_kernel(tc, X, A, W_in_words, W_in_scales, b_in, eps0, out):
     nc = tc.nc
 
     x_view = X.rearrange("(g q p e) k -> g p q (e k)", g=PASSES, q=2, p=P, e=2)
-    a_view = A.rearrange("(d p e) k -> d p (e k)", d=A_LOADS, p=P, e=2)
-    out_view = out.rearrange("(d p e) n -> d p (e n)", d=A_LOADS, p=P, e=2)
+    a_view = A.rearrange("(d p e) k -> d p e k", d=A_LOADS, p=P, e=2)
+    out_view = out.rearrange("(d p e) n -> p d (e n)", d=A_LOADS, p=P, e=2)
 
     with ExitStack() as ctx:
         const = ctx.enter_context(tc.tile_pool(name="const", bufs=1))
         x_pool = ctx.enter_context(tc.tile_pool(name="x_rows", bufs=PASSES))
         a_pool = ctx.enter_context(tc.tile_pool(name="a_rows", bufs=A_BUFS))
         grouped_pool = ctx.enter_context(
-            tc.tile_pool(name="grouped", bufs=2 * ROW_TILES_PER_ROUND + 1)
+            tc.tile_pool(name="grouped", bufs=3)
         )
-        mx_pool = ctx.enter_context(tc.tile_pool(name="mx", bufs=2 * ROW_TILES_PER_ROUND + 1))
-        result_pool = ctx.enter_context(tc.tile_pool(name="result", bufs=A_LOADS))
+        mx_pool = ctx.enter_context(tc.tile_pool(name="mx", bufs=3))
         transposed_banks = ctx.enter_context(tc.psum_pool(name="transposed", bufs=6))
         sum_banks = ctx.enter_context(tc.psum_pool(name="sums", bufs=2))
         ctx.enter_context(tc.manual_schedule())
@@ -73,21 +72,35 @@ def tile_gin_pa_t_kernel(tc, X, A, W_in_words, W_in_scales, b_in, eps0, out):
             out=w_codes[:].bitcast(I32),
             in_=W_in_words[0].rearrange("p n t -> p (n t)").bitcast(I32),
         )
-        small_rows = const.tile([P, 2 * HID], BF16, name="small_rows")
-        nc.vector.memset(small_rows[:], 0.0)
-        nc.scalar.dma_start(out=small_rows[0:1, 0:HID], in_=b_in.unsqueeze(0))
-        nc.scalar.dma_start(out=small_rows[0:1, HID : HID + 1], in_=eps0.unsqueeze(0))
+        bias_row = const.tile([P, HID], BF16, name="bias_row")
+        eps_row = const.tile([P, 2], BF16, name="eps_row")
+        nc.vector.memset(bias_row[:], 0.0)
+        nc.vector.memset(eps_row[:], 0.0)
+        nc.scalar.dma_start(out=bias_row[0:1, :], in_=b_in.unsqueeze(0))
 
         for g in range(1, PASSES):
             load_x(g)
+        nc.sync.dma_start(out=eps_row[0:1, 0:1], in_=eps0.unsqueeze(0))
+
+        units = [(r, 0, PASSES) for r in range(NODE_TILES - 2)]
+        units += [(NODE_TILES - 2, c, PASSES // 2) for c in range(0, PASSES, PASSES // 2)]
+        units += [(NODE_TILES - 1, c, PASSES // 4) for c in range(0, PASSES, PASSES // 4)]
 
         a_rows = []
 
         def load_a():
+            d = len(a_rows)
             rows = a_pool.tile([P, 2, NODES], BF16, name="a_rows")
-            nc.sync.dma_start(
-                out=rows[:].rearrange("p e k -> p (e k)"), in_=a_view[len(a_rows)]
-            )
+            if d < A_LOADS - 1:
+                nc.sync.dma_start(
+                    out=rows[:].rearrange("p e k -> p (e k)"),
+                    in_=a_view[d].rearrange("p e k -> p (e k)"),
+                )
+            else:
+                for r, c, n in units:
+                    if r // 2 == d:
+                        k = slice(c * K_PASS, (c + n) * K_PASS)
+                        nc.sync.dma_start(out=rows[:, r % 2, k], in_=a_view[d, :, r % 2, k])
             a_rows.append(rows)
 
         for d in range(A_BUFS):
@@ -95,14 +108,18 @@ def tile_gin_pa_t_kernel(tc, X, A, W_in_words, W_in_scales, b_in, eps0, out):
 
         ones = const.tile([P, P], BF16, name="ones")
         nc.vector.memset(ones[:], 1.0)
-        spread = sum_banks.tile([P, 2 * HID], F32, name="spread", tag="sums")
-        nc.tensor.matmul(out=spread[:], lhsT=ones[:], rhs=small_rows[:], start=True, stop=True)
         bias = const.tile([P, HID], F32, name="bias")
-        nc.vector.tensor_copy(out=bias[:], in_=spread[:, 0:HID])
         self_weight = const.tile([P, 1], F32, name="self_weight")
-        nc.vector.tensor_scalar_add(
-            out=self_weight[:], in0=spread[:, HID : HID + 1], scalar1=1.0
-        )
+
+        def spread_bias():
+            spread = sum_banks.tile([P, HID], F32, name="bias_sum", tag="sums")
+            nc.tensor.matmul(out=spread[:], lhsT=ones[:], rhs=bias_row[:], start=True, stop=True)
+            nc.vector.tensor_copy(out=bias[:], in_=spread[:])
+
+        def spread_eps():
+            spread = sum_banks.tile([P, 2], F32, name="eps_sum", tag="sums")
+            nc.tensor.matmul(out=spread[:], lhsT=ones[:], rhs=eps_row[:], start=True, stop=True)
+            nc.vector.tensor_scalar_add(out=self_weight[:], in0=spread[:, 0:1], scalar1=1.0)
 
         h_f32 = const.tile([P, NODE_TILES, HID], F32, name="h_f32")
         h_grouped = const.tile([P, PASSES, HID, PACK], BF16, name="h_grouped", align_bytes=64)
@@ -178,74 +195,95 @@ def tile_gin_pa_t_kernel(tc, X, A, W_in_words, W_in_scales, b_in, eps0, out):
                 x_grouped[turn] = transpose_and_group(x_word_block(turn), PACK, vector_banks=1)
             if 0 <= turn - 1 < PASSES:
                 x_mx[turn - 1] = quantise(x_grouped[turn - 1], PACK)
+            if turn == 1:
+                spread_bias()
             if 0 <= turn - 2 < PASSES:
                 project(turn - 2, x_mx[turn - 2][0], x_mx[turn - 2][1])
             if 0 <= turn - 3 < PASSES:
                 quantise_h(turn - 3)
 
-        def a_word_block(r):
+        def a_word_block(r, first):
             words = a_rows[r // 2][:].bitcast(F32)
-            return lambda c, v: words[:, r % 2, (2 * c + v) * P : (2 * c + v + 1) * P]
+            def word_block(i, v):
+                start = (2 * (first + i) + v) * P
+                return words[:, r % 2, start : start + P]
 
+            return word_block
+
+        results = const.tile([P, NODE_TILES, HID], F32, name="results")
         out_sums = {}
-        results = {}
 
-        def store(d):
-            nc.sync.dma_start(out=out_view[d], in_=results[d][:].rearrange("p e n -> p (e n)"))
-
-        def aggregate(r, codes, scales):
-            d, e = divmod(r, 2)
-            if e == 0:
-                out_sums[d] = sum_banks.tile([P, 2, HID], F32, name="out_sum", tag="sums")
-            for c in range(PASSES):
-                cols = slice(c * P, (c + 1) * P)
+        def aggregate(unit, codes, scales):
+            r, first, n = unit
+            if r not in out_sums:
+                if r < NODE_TILES - 2:
+                    bank = sum_banks.tile([P, 2, HID], F32, name="out_sum", tag="sums")
+                    out_sums[r], out_sums[r + 1] = bank[:, 0, :], bank[:, 1, :]
+                    out_sums[r, r + 1] = bank[:]
+                else:
+                    bank = sum_banks.tile([P, HID], F32, name="last_sum", tag="sums")
+                    out_sums[r] = bank[:]
+            for i in range(n):
+                cols = slice(i * P, (i + 1) * P)
+                c = first + i
+                h_cols = slice(c * HID, (c + 1) * HID)
                 nc.tensor.matmul_mx(
-                    out=out_sums[d][:, e, :],
+                    out=out_sums[r],
                     lhsT=codes[:, cols].bitcast(FP8X4),
                     lhsT_scale=scales[:, cols],
-                    rhs=h_codes[:, cols].bitcast(FP8X4),
-                    rhs_scale=h_scales[:, cols],
+                    rhs=h_codes[:, h_cols].bitcast(FP8X4),
+                    rhs_scale=h_scales[:, h_cols],
                     start=(c == 0),
                     stop=(c == PASSES - 1),
                 )
-            if e == 1:
-                results[d] = result_pool.tile([P, 2, HID], F32, name="result")
-                nc.vector.scalar_tensor_tensor(
-                    out=results[d][:],
-                    in0=h_f32[:, 2 * d : 2 * d + 2, :],
-                    scalar=self_weight[:, 0:1],
-                    in1=out_sums[d][:],
-                    op0=MULT,
-                    op1=ADD,
+
+        def add_self_term(r0, r1, sums):
+            nc.vector.scalar_tensor_tensor(
+                out=results[:, r0:r1, :],
+                in0=h_f32[:, r0:r1, :],
+                scalar=self_weight[:, 0:1],
+                in1=sums,
+                op0=MULT,
+                op1=ADD,
+            )
+
+        stored = 0
+
+        def store(r0, r1):
+            if r1 - r0 == 1:
+                cols = slice(r0 % 2 * HID, (r0 % 2 + 1) * HID)
+                nc.sync.dma_start(out=out_view[:, r0 // 2, cols], in_=results[:, r0, :])
+            else:
+                nc.sync.dma_start(
+                    out=out_view[:, r0 // 2 : r1 // 2, :],
+                    in_=results[:, r0:r1, :].rearrange("p (d e) n -> p d (e n)", e=2),
                 )
-                if len(a_rows) == A_LOADS:
-                    store(d)
-
-        def load_next_a():
-            if len(a_rows) < A_LOADS:
-                load_a()
-                if len(a_rows) == A_LOADS:
-                    for d in sorted(results):
-                        store(d)
-
-        rounds = NODE_TILES // ROW_TILES_PER_ROUND
-
-        def row_tiles(turn):
-            return range(turn * ROW_TILES_PER_ROUND, (turn + 1) * ROW_TILES_PER_ROUND)
 
         a_grouped = {}
         a_mx = {}
-        for turn in range(rounds + 2):
-            if turn < rounds:
-                for r in row_tiles(turn):
-                    a_grouped[r] = transpose_and_group(
-                        a_word_block(r), PASSES, vector_banks=r % 2
-                    )
-                    if r % 2 == 1:
-                        load_next_a()
-            if 0 <= turn - 1 < rounds:
-                for r in row_tiles(turn - 1):
-                    a_mx[r] = quantise(a_grouped[r], PASSES)
-            if 0 <= turn - 2 < rounds:
-                for r in row_tiles(turn - 2):
-                    aggregate(r, a_mx[r][0], a_mx[r][1])
+        for turn in range(len(units) + 2):
+            if turn == 0:
+                spread_eps()
+            if turn < len(units):
+                r, c, n = units[turn]
+                vector_banks = 1 if n > 2 else c // n % 2
+                a_grouped[turn] = transpose_and_group(
+                    a_word_block(r, c), n, vector_banks=vector_banks
+                )
+                if r % 2 == 1 and len(a_rows) < A_LOADS:
+                    load_a()
+            if 0 <= turn - 1 < len(units):
+                a_mx[turn - 1] = quantise(a_grouped[turn - 1], units[turn - 1][2])
+            if 0 <= turn - 2 < len(units):
+                r, c, n = units[turn - 2]
+                aggregate(units[turn - 2], a_mx[turn - 2][0], a_mx[turn - 2][1])
+                if c + n == PASSES:
+                    if r >= NODE_TILES - 2:
+                        add_self_term(r, r + 1, out_sums[r].unsqueeze(1))
+                        store(r, r + 1)
+                    elif r % 2 == 1:
+                        add_self_term(r - 1, r + 1, out_sums[r - 1, r])
+                        ready = r % STORE_TILES == STORE_TILES - 1 or r == NODE_TILES - 3
+                        if ready and len(a_rows) == A_LOADS:
+                            store(stored, r + 1)
+                            stored = r + 1

@@ -20,9 +20,9 @@ IN_DIM = 512
 HID = 128
 NODE_TILES = NODES // P
 PASSES = NODES // K_PASS
-A_LOADS = NODE_TILES // 2
-A_BUFS = 5
-STORE_TILES = 4
+PAIRS = NODE_TILES // 2
+A_BUFS = 10
+STORE_PAIRS = 2
 
 FLOPS = 2 * NODES * IN_DIM * HID + 2 * NODES * NODES * HID
 
@@ -31,8 +31,8 @@ def tile_gin_pa_t_kernel(tc, X, A, W_in_words, W_in_scales, b_in, eps0, out):
     nc = tc.nc
 
     x_view = X.rearrange("(g q p e) k -> g p q (e k)", g=PASSES, q=2, p=P, e=2)
-    a_view = A.rearrange("(d p e) k -> d p e k", d=A_LOADS, p=P, e=2)
-    out_view = out.rearrange("(d p e) n -> p d (e n)", d=A_LOADS, p=P, e=2)
+    a_view = A.rearrange("(d p e) k -> d p e k", d=PAIRS, p=P, e=2)
+    out_view = out.rearrange("(d p e) n -> p d (e n)", d=PAIRS, p=P, e=2)
 
     with ExitStack() as ctx:
         const = ctx.enter_context(tc.tile_pool(name="const", bufs=1))
@@ -82,25 +82,12 @@ def tile_gin_pa_t_kernel(tc, X, A, W_in_words, W_in_scales, b_in, eps0, out):
             load_x(g)
         nc.sync.dma_start(out=eps_row[0:1, 0:1], in_=eps0.unsqueeze(0))
 
-        units = [(r, 0, PASSES) for r in range(NODE_TILES - 2)]
-        units += [(NODE_TILES - 2, c, PASSES // 2) for c in range(0, PASSES, PASSES // 2)]
-        units += [(NODE_TILES - 1, c, PASSES // 4) for c in range(0, PASSES, PASSES // 4)]
-
         a_rows = []
 
         def load_a():
-            d = len(a_rows)
-            rows = a_pool.tile([P, 2, NODES], BF16, name="a_rows")
-            if d < A_LOADS - 1:
-                nc.sync.dma_start(
-                    out=rows[:].rearrange("p e k -> p (e k)"),
-                    in_=a_view[d].rearrange("p e k -> p (e k)"),
-                )
-            else:
-                for r, c, n in units:
-                    if r // 2 == d:
-                        k = slice(c * K_PASS, (c + n) * K_PASS)
-                        nc.sync.dma_start(out=rows[:, r % 2, k], in_=a_view[d, :, r % 2, k])
+            d, e = divmod(len(a_rows), 2)
+            rows = a_pool.tile([P, NODES], BF16, name="a_rows")
+            nc.sync.dma_start(out=rows[:], in_=a_view[d, :, e, :])
             a_rows.append(rows)
 
         for d in range(A_BUFS):
@@ -202,88 +189,66 @@ def tile_gin_pa_t_kernel(tc, X, A, W_in_words, W_in_scales, b_in, eps0, out):
             if 0 <= turn - 3 < PASSES:
                 quantise_h(turn - 3)
 
-        def a_word_block(r, first):
-            words = a_rows[r // 2][:].bitcast(F32)
-            def word_block(i, v):
-                start = (2 * (first + i) + v) * P
-                return words[:, r % 2, start : start + P]
-
-            return word_block
+        def a_word_block(r):
+            words = a_rows[r][:].bitcast(F32)
+            return lambda c, v: words[:, (2 * c + v) * P : (2 * c + v + 1) * P]
 
         results = const.tile([P, NODE_TILES, HID], F32, name="results")
         out_sums = {}
 
-        def aggregate(unit, codes, scales):
-            r, first, n = unit
-            if r not in out_sums:
-                if r < NODE_TILES - 2:
-                    bank = sum_banks.tile([P, 2, HID], F32, name="out_sum", tag="sums")
-                    out_sums[r], out_sums[r + 1] = bank[:, 0, :], bank[:, 1, :]
-                    out_sums[r, r + 1] = bank[:]
-                else:
-                    bank = sum_banks.tile([P, HID], F32, name="last_sum", tag="sums")
-                    out_sums[r] = bank[:]
-            for i in range(n):
-                cols = slice(i * P, (i + 1) * P)
-                c = first + i
-                h_cols = slice(c * HID, (c + 1) * HID)
+        def aggregate(r, codes, scales):
+            if r % 2 == 0:
+                out_sums[r // 2] = sum_banks.tile([P, 2, HID], F32, name="out_sum", tag="sums")
+            for c in range(PASSES):
+                cols = slice(c * P, (c + 1) * P)
                 nc.tensor.matmul_mx(
-                    out=out_sums[r],
+                    out=out_sums[r // 2][:, r % 2, :],
                     lhsT=codes[:, cols].bitcast(FP8X4),
                     lhsT_scale=scales[:, cols],
-                    rhs=h_codes[:, h_cols].bitcast(FP8X4),
-                    rhs_scale=h_scales[:, h_cols],
+                    rhs=h_codes[:, cols].bitcast(FP8X4),
+                    rhs_scale=h_scales[:, cols],
                     start=(c == 0),
                     stop=(c == PASSES - 1),
                 )
 
-        def add_self_term(r0, r1, sums):
+        def add_self_term(d):
+            tiles = slice(2 * d, 2 * d + 2)
             nc.vector.scalar_tensor_tensor(
-                out=results[:, r0:r1, :],
-                in0=h_f32[:, r0:r1, :],
+                out=results[:, tiles, :],
+                in0=h_f32[:, tiles, :],
                 scalar=self_weight[:, 0:1],
-                in1=sums,
+                in1=out_sums[d][:],
                 op0=MULT,
                 op1=ADD,
             )
 
+        def store(d0, d1):
+            nc.sync.dma_start(
+                out=out_view[:, d0:d1, :],
+                in_=results[:, 2 * d0 : 2 * d1, :].rearrange("p (d e) n -> p d (e n)", e=2),
+            )
+
         stored = 0
-
-        def store(r0, r1):
-            if r1 - r0 == 1:
-                cols = slice(r0 % 2 * HID, (r0 % 2 + 1) * HID)
-                nc.sync.dma_start(out=out_view[:, r0 // 2, cols], in_=results[:, r0, :])
-            else:
-                nc.sync.dma_start(
-                    out=out_view[:, r0 // 2 : r1 // 2, :],
-                    in_=results[:, r0:r1, :].rearrange("p (d e) n -> p d (e n)", e=2),
-                )
-
         a_grouped = {}
         a_mx = {}
-        for turn in range(len(units) + 2):
+        for turn in range(NODE_TILES + 2):
             if turn == 0:
                 spread_eps()
-            if turn < len(units):
-                r, c, n = units[turn]
-                vector_banks = 1 if n > 2 else c // n % 2
+            if turn < NODE_TILES:
                 a_grouped[turn] = transpose_and_group(
-                    a_word_block(r, c), n, vector_banks=vector_banks
+                    a_word_block(turn), PASSES, vector_banks=1
                 )
-                if r % 2 == 1 and len(a_rows) < A_LOADS:
+                if len(a_rows) < NODE_TILES:
                     load_a()
-            if 0 <= turn - 1 < len(units):
-                a_mx[turn - 1] = quantise(a_grouped[turn - 1], units[turn - 1][2])
-            if 0 <= turn - 2 < len(units):
-                r, c, n = units[turn - 2]
-                aggregate(units[turn - 2], a_mx[turn - 2][0], a_mx[turn - 2][1])
-                if c + n == PASSES:
-                    if r >= NODE_TILES - 2:
-                        add_self_term(r, r + 1, out_sums[r].unsqueeze(1))
-                        store(r, r + 1)
-                    elif r % 2 == 1:
-                        add_self_term(r - 1, r + 1, out_sums[r - 1, r])
-                        ready = r % STORE_TILES == STORE_TILES - 1 or r == NODE_TILES - 3
-                        if ready and len(a_rows) == A_LOADS:
-                            store(stored, r + 1)
-                            stored = r + 1
+            if 0 <= turn - 1 < NODE_TILES:
+                a_mx[turn - 1] = quantise(a_grouped[turn - 1], PASSES)
+            if 0 <= turn - 2 < NODE_TILES:
+                r = turn - 2
+                aggregate(r, a_mx[r][0], a_mx[r][1])
+                d, e = divmod(r, 2)
+                if e == 1:
+                    add_self_term(d)
+                    full = d % STORE_PAIRS == STORE_PAIRS - 1 or d >= PAIRS - 2
+                    if full and len(a_rows) == NODE_TILES:
+                        store(stored, d + 1)
+                        stored = d + 1

@@ -21,8 +21,9 @@ HID = 128
 NODE_TILES = NODES // P
 PASSES = NODES // K_PASS
 PAIRS = NODE_TILES // 2
-A_BUFS = 10
-STORE_PAIRS = 2
+A_BUFS = 5
+SPLIT_PAIRS = 3
+STORE_TILES = 4
 
 FLOPS = 2 * NODES * IN_DIM * HID + 2 * NODES * NODES * HID
 
@@ -84,10 +85,23 @@ def tile_gin_pa_t_kernel(tc, X, A, W_in_words, W_in_scales, b_in, eps0, out):
 
         a_rows = []
 
+        LAST = NODE_TILES - 1
+        units = [(r, 0, PASSES) for r in range(LAST)]
+        last_units = [(LAST, 0, 4), (LAST, 4, 2), (LAST, 6, 2)]
+
         def load_a():
-            d, e = divmod(len(a_rows), 2)
-            rows = a_pool.tile([P, NODES], BF16, name="a_rows")
-            nc.sync.dma_start(out=rows[:], in_=a_view[d, :, e, :])
+            d = len(a_rows)
+            rows = a_pool.tile([P, 2, NODES], BF16, name="a_rows")
+            if d < PAIRS - SPLIT_PAIRS:
+                nc.sync.dma_start(
+                    out=rows[:].rearrange("p e k -> p (e k)"),
+                    in_=a_view[d].rearrange("p e k -> p (e k)"),
+                )
+            else:
+                for r, first, n in units + last_units:
+                    if r // 2 == d:
+                        k = slice(first * K_PASS, (first + n) * K_PASS)
+                        nc.sync.dma_start(out=rows[:, r % 2, k], in_=a_view[d, :, r % 2, k])
             a_rows.append(rows)
 
         for d in range(A_BUFS):
@@ -189,66 +203,100 @@ def tile_gin_pa_t_kernel(tc, X, A, W_in_words, W_in_scales, b_in, eps0, out):
             if 0 <= turn - 3 < PASSES:
                 quantise_h(turn - 3)
 
-        def a_word_block(r):
-            words = a_rows[r][:].bitcast(F32)
-            return lambda c, v: words[:, (2 * c + v) * P : (2 * c + v + 1) * P]
+        def a_word_block(r, first):
+            words = a_rows[r // 2][:].bitcast(F32)
+            def word_block(i, v):
+                start = (2 * (first + i) + v) * P
+                return words[:, r % 2, start : start + P]
+
+            return word_block
 
         results = const.tile([P, NODE_TILES, HID], F32, name="results")
         out_sums = {}
+        a_grouped = {}
+        a_mx = {}
 
-        def aggregate(r, codes, scales):
-            if r % 2 == 0:
-                out_sums[r // 2] = sum_banks.tile([P, 2, HID], F32, name="out_sum", tag="sums")
-            for c in range(PASSES):
-                cols = slice(c * P, (c + 1) * P)
+        def transpose_unit(unit):
+            r, first, n = unit
+            a_grouped[unit] = transpose_and_group(
+                a_word_block(r, first), n, vector_banks=1 if n == PASSES else 0
+            )
+            if r % 2 == 1 and len(a_rows) < PAIRS:
+                load_a()
+
+        def quantise_unit(unit):
+            a_mx[unit] = quantise(a_grouped[unit], unit[2])
+
+        def aggregate_unit(unit):
+            r, first, n = unit
+            codes, scales = a_mx[unit]
+            shared = r < NODE_TILES - 2
+            if first == 0:
+                if not shared:
+                    bank = sum_banks.tile([P, 1, HID], F32, name="last_sum", tag="sums")
+                    out_sums[r] = (bank, 0)
+                elif r % 2 == 0:
+                    bank = sum_banks.tile([P, 2, HID], F32, name="out_sum", tag="sums")
+                    out_sums[r], out_sums[r + 1] = (bank, 0), (bank, 1)
+            bank, slot = out_sums[r]
+            for i in range(n):
+                c = first + i
+                cols = slice(i * P, (i + 1) * P)
+                h_cols = slice(c * HID, (c + 1) * HID)
                 nc.tensor.matmul_mx(
-                    out=out_sums[r // 2][:, r % 2, :],
+                    out=bank[:, slot, :],
                     lhsT=codes[:, cols].bitcast(FP8X4),
                     lhsT_scale=scales[:, cols],
-                    rhs=h_codes[:, cols].bitcast(FP8X4),
-                    rhs_scale=h_scales[:, cols],
+                    rhs=h_codes[:, h_cols].bitcast(FP8X4),
+                    rhs_scale=h_scales[:, h_cols],
                     start=(c == 0),
                     stop=(c == PASSES - 1),
                 )
+            if first + n == PASSES and (r % 2 == 1 or not shared):
+                finish(r - 1 if shared else r, r + 1, bank)
 
-        def add_self_term(d):
-            tiles = slice(2 * d, 2 * d + 2)
+        def finish(r0, r1, bank):
             nc.vector.scalar_tensor_tensor(
-                out=results[:, tiles, :],
-                in0=h_f32[:, tiles, :],
+                out=results[:, r0:r1, :],
+                in0=h_f32[:, r0:r1, :],
                 scalar=self_weight[:, 0:1],
-                in1=out_sums[d][:],
+                in1=bank[:],
                 op0=MULT,
                 op1=ADD,
             )
+            due = r1 % STORE_TILES == 0 or r1 >= NODE_TILES - 2
+            if due and len(a_rows) == PAIRS:
+                store(stored_to[0], r1)
+                stored_to[0] = r1
 
-        def store(d0, d1):
-            nc.sync.dma_start(
-                out=out_view[:, d0:d1, :],
-                in_=results[:, 2 * d0 : 2 * d1, :].rearrange("p (d e) n -> p d (e n)", e=2),
-            )
+        stored_to = [0]
 
-        stored = 0
-        a_grouped = {}
-        a_mx = {}
-        for turn in range(NODE_TILES + 2):
-            if turn == 0:
-                spread_eps()
-            if turn < NODE_TILES:
-                a_grouped[turn] = transpose_and_group(
-                    a_word_block(turn), PASSES, vector_banks=1
+        def store(r0, r1):
+            if r1 - r0 == 1:
+                cols = slice(r0 % 2 * HID, (r0 % 2 + 1) * HID)
+                nc.sync.dma_start(out=out_view[:, r0 // 2, cols], in_=results[:, r0, :])
+            else:
+                nc.sync.dma_start(
+                    out=out_view[:, r0 // 2 : r1 // 2, :],
+                    in_=results[:, r0:r1, :].rearrange("p (d e) n -> p d (e n)", e=2),
                 )
-                if len(a_rows) < NODE_TILES:
-                    load_a()
-            if 0 <= turn - 1 < NODE_TILES:
-                a_mx[turn - 1] = quantise(a_grouped[turn - 1], PASSES)
-            if 0 <= turn - 2 < NODE_TILES:
-                r = turn - 2
-                aggregate(r, a_mx[r][0], a_mx[r][1])
-                d, e = divmod(r, 2)
-                if e == 1:
-                    add_self_term(d)
-                    full = d % STORE_PAIRS == STORE_PAIRS - 1 or d >= PAIRS - 2
-                    if full and len(a_rows) == NODE_TILES:
-                        store(stored, d + 1)
-                        stored = d + 1
+
+        spread_eps()
+        for turn, unit in enumerate(units):
+            transpose_unit(unit)
+            if turn >= 1:
+                quantise_unit(units[turn - 1])
+            if turn >= 2:
+                aggregate_unit(units[turn - 2])
+        transpose_unit(last_units[0])
+        quantise_unit(units[-1])
+        aggregate_unit(units[-2])
+        for before, unit in zip(last_units, last_units[1:]):
+            transpose_unit(unit)
+            quantise_unit(before)
+        aggregate_unit(units[-1])
+        for unit in last_units[:-2]:
+            aggregate_unit(unit)
+        quantise_unit(last_units[-1])
+        for unit in last_units[-2:]:
+            aggregate_unit(unit)

@@ -21,8 +21,7 @@ HID = 128
 NODE_TILES = NODES // P
 PASSES = NODES // K_PASS
 PAIRS = NODE_TILES // 2
-A_BUFS = 5
-SPLIT_PAIRS = 3
+A_BUFS = 10
 STORE_TILES = 4
 
 FLOPS = 2 * NODES * IN_DIM * HID + 2 * NODES * NODES * HID
@@ -90,18 +89,12 @@ def tile_gin_pa_t_kernel(tc, X, A, W_in_words, W_in_scales, b_in, eps0, out):
         last_units = [(LAST, 0, 4), (LAST, 4, 2), (LAST, 6, 2)]
 
         def load_a():
-            d = len(a_rows)
-            rows = a_pool.tile([P, 2, NODES], BF16, name="a_rows")
-            if d < PAIRS - SPLIT_PAIRS:
-                nc.sync.dma_start(
-                    out=rows[:].rearrange("p e k -> p (e k)"),
-                    in_=a_view[d].rearrange("p e k -> p (e k)"),
-                )
-            else:
-                for r, first, n in units + last_units:
-                    if r // 2 == d:
-                        k = slice(first * K_PASS, (first + n) * K_PASS)
-                        nc.sync.dma_start(out=rows[:, r % 2, k], in_=a_view[d, :, r % 2, k])
+            d, e = divmod(len(a_rows), 2)
+            rows = a_pool.tile([P, NODES], BF16, name="a_rows")
+            for r, first, n in units + last_units:
+                if r == len(a_rows):
+                    k = slice(first * K_PASS, (first + n) * K_PASS)
+                    nc.sync.dma_start(out=rows[:, k], in_=a_view[d, :, e, k])
             a_rows.append(rows)
 
         for d in range(A_BUFS):
@@ -204,10 +197,10 @@ def tile_gin_pa_t_kernel(tc, X, A, W_in_words, W_in_scales, b_in, eps0, out):
                 quantise_h(turn - 3)
 
         def a_word_block(r, first):
-            words = a_rows[r // 2][:].bitcast(F32)
+            words = a_rows[r][:].bitcast(F32)
             def word_block(i, v):
                 start = (2 * (first + i) + v) * P
-                return words[:, r % 2, start : start + P]
+                return words[:, start : start + P]
 
             return word_block
 
@@ -221,7 +214,7 @@ def tile_gin_pa_t_kernel(tc, X, A, W_in_words, W_in_scales, b_in, eps0, out):
             a_grouped[unit] = transpose_and_group(
                 a_word_block(r, first), n, vector_banks=1 if n == PASSES else 0
             )
-            if r % 2 == 1 and len(a_rows) < PAIRS:
+            if len(a_rows) < NODE_TILES:
                 load_a()
 
         def quantise_unit(unit):
@@ -265,7 +258,7 @@ def tile_gin_pa_t_kernel(tc, X, A, W_in_words, W_in_scales, b_in, eps0, out):
                 op1=ADD,
             )
             due = r1 % STORE_TILES == 0 or r1 >= NODE_TILES - 2
-            if due and len(a_rows) == PAIRS:
+            if due and len(a_rows) == NODE_TILES:
                 store(stored_to[0], r1)
                 stored_to[0] = r1
 

@@ -39,9 +39,9 @@ def tile_gin_pa_t_kernel(tc, X, A, W_in_words, W_in_scales, b_in, eps0, out):
         x_pool = ctx.enter_context(tc.tile_pool(name="x_rows", bufs=PASSES))
         a_pool = ctx.enter_context(tc.tile_pool(name="a_rows", bufs=A_BUFS))
         grouped_pool = ctx.enter_context(
-            tc.tile_pool(name="grouped", bufs=3)
+            tc.tile_pool(name="grouped", bufs=4)
         )
-        mx_pool = ctx.enter_context(tc.tile_pool(name="mx", bufs=3))
+        mx_pool = ctx.enter_context(tc.tile_pool(name="mx", bufs=6))
         transposed_banks = ctx.enter_context(tc.psum_pool(name="transposed", bufs=6))
         sum_banks = ctx.enter_context(tc.psum_pool(name="sums", bufs=2))
         ctx.enter_context(tc.manual_schedule())
@@ -60,6 +60,18 @@ def tile_gin_pa_t_kernel(tc, X, A, W_in_words, W_in_scales, b_in, eps0, out):
 
         load_x(0)
 
+        bias_row = const.tile([P, HID], BF16, name="bias_row")
+        eps_row = const.tile([P, 2], BF16, name="eps_row")
+        nc.vector.memset(bias_row[:], 0.0)
+        nc.vector.memset(eps_row[:], 0.0)
+        nc.sync.dma_start(out=bias_row[0:1, :], in_=b_in.unsqueeze(0))
+        w_codes = const.tile([P, HID * PACK], U8, name="w_codes", align_bytes=64)
+        nc.sync.dma_start(
+            out=w_codes[:].bitcast(I32),
+            in_=W_in_words[0].rearrange("p n t -> p (n t)").bitcast(I32),
+        )
+        load_x(1)
+        load_x(2)
         w_scales = const.tile([P, HID], U8, name="w_scales", align_bytes=64)
         nc.vector.memset(w_scales[:].bitcast(I32), 0)
         for quadrant in range(4):
@@ -67,31 +79,21 @@ def tile_gin_pa_t_kernel(tc, X, A, W_in_words, W_in_scales, b_in, eps0, out):
                 out=w_scales[32 * quadrant : 32 * quadrant + 4, :].bitcast(I32),
                 in_=W_in_scales[0, 4 * quadrant : 4 * quadrant + 4, :].bitcast(I32),
             )
-        w_codes = const.tile([P, HID * PACK], U8, name="w_codes", align_bytes=64)
-        nc.sync.dma_start(
-            out=w_codes[:].bitcast(I32),
-            in_=W_in_words[0].rearrange("p n t -> p (n t)").bitcast(I32),
-        )
-        bias_row = const.tile([P, HID], BF16, name="bias_row")
-        eps_row = const.tile([P, 2], BF16, name="eps_row")
-        nc.vector.memset(bias_row[:], 0.0)
-        nc.vector.memset(eps_row[:], 0.0)
-        nc.scalar.dma_start(out=bias_row[0:1, :], in_=b_in.unsqueeze(0))
-
-        for g in range(1, PASSES):
+        for g in range(3, PASSES):
             load_x(g)
         nc.sync.dma_start(out=eps_row[0:1, 0:1], in_=eps0.unsqueeze(0))
 
         a_rows = []
 
         LAST = NODE_TILES - 1
-        units = [(r, 0, PASSES) for r in range(LAST)]
-        last_units = [(LAST, 0, 4), (LAST, 4, 2), (LAST, 6, 2)]
+        units = [(r, 0, PASSES) for r in range(LAST - 1)]
+        next_to_last = [(LAST - 1, 0, 4), (LAST - 1, 4, 4)]
+        last = [(LAST, 0, 4), (LAST, 4, 2), (LAST, 6, 2)]
 
         def load_a():
             d, e = divmod(len(a_rows), 2)
             rows = a_pool.tile([P, NODES], BF16, name="a_rows")
-            for r, first, n in units + last_units:
+            for r, first, n in units + next_to_last + last:
                 if r == len(a_rows):
                     k = slice(first * K_PASS, (first + n) * K_PASS)
                     nc.sync.dma_start(out=rows[:, k], in_=a_view[d, :, e, k])
@@ -212,7 +214,7 @@ def tile_gin_pa_t_kernel(tc, X, A, W_in_words, W_in_scales, b_in, eps0, out):
         def transpose_unit(unit):
             r, first, n = unit
             a_grouped[unit] = transpose_and_group(
-                a_word_block(r, first), n, vector_banks=1 if n == PASSES else 0
+                a_word_block(r, first), n, vector_banks=1 if first == 0 and r < LAST else 0
             )
             if len(a_rows) < NODE_TILES:
                 load_a()
@@ -281,15 +283,18 @@ def tile_gin_pa_t_kernel(tc, X, A, W_in_words, W_in_scales, b_in, eps0, out):
                 quantise_unit(units[turn - 1])
             if turn >= 2:
                 aggregate_unit(units[turn - 2])
-        transpose_unit(last_units[0])
+        for unit in next_to_last:
+            transpose_unit(unit)
         quantise_unit(units[-1])
         aggregate_unit(units[-2])
-        for before, unit in zip(last_units, last_units[1:]):
+        for unit in last[:-1]:
             transpose_unit(unit)
-            quantise_unit(before)
+        for unit in next_to_last:
+            quantise_unit(unit)
+        transpose_unit(last[-1])
+        quantise_unit(last[0])
         aggregate_unit(units[-1])
-        for unit in last_units[:-2]:
-            aggregate_unit(unit)
-        quantise_unit(last_units[-1])
-        for unit in last_units[-2:]:
+        for unit in last[1:]:
+            quantise_unit(unit)
+        for unit in next_to_last + last:
             aggregate_unit(unit)

@@ -21,7 +21,8 @@ HID = 128
 NODE_TILES = NODES // P
 PASSES = NODES // K_PASS
 PAIRS = NODE_TILES // 2
-A_BUFS = 10
+A_BUFS = 5
+WHOLE_PAIRS = 8
 STORE_TILES = 4
 
 FLOPS = 2 * NODES * IN_DIM * HID + 2 * NODES * NODES * HID
@@ -91,12 +92,18 @@ def tile_gin_pa_t_kernel(tc, X, A, W_in_words, W_in_scales, b_in, eps0, out):
         last = [(LAST, 0, 4), (LAST, 4, 2), (LAST, 6, 2)]
 
         def load_a():
-            d, e = divmod(len(a_rows), 2)
-            rows = a_pool.tile([P, NODES], BF16, name="a_rows")
-            for r, first, n in units + next_to_last + last:
-                if r == len(a_rows):
-                    k = slice(first * K_PASS, (first + n) * K_PASS)
-                    nc.sync.dma_start(out=rows[:, k], in_=a_view[d, :, e, k])
+            d = len(a_rows)
+            rows = a_pool.tile([P, 2, NODES], BF16, name="a_rows")
+            if d < WHOLE_PAIRS:
+                nc.sync.dma_start(
+                    out=rows[:].rearrange("p e k -> p (e k)"),
+                    in_=a_view[d].rearrange("p e k -> p (e k)"),
+                )
+            else:
+                for r, first, n in units + next_to_last + last:
+                    if r // 2 == d:
+                        k = slice(first * K_PASS, (first + n) * K_PASS)
+                        nc.sync.dma_start(out=rows[:, r % 2, k], in_=a_view[d, :, r % 2, k])
             a_rows.append(rows)
 
         for d in range(A_BUFS):
@@ -199,10 +206,10 @@ def tile_gin_pa_t_kernel(tc, X, A, W_in_words, W_in_scales, b_in, eps0, out):
                 quantise_h(turn - 3)
 
         def a_word_block(r, first):
-            words = a_rows[r][:].bitcast(F32)
+            words = a_rows[r // 2][:].bitcast(F32)
             def word_block(i, v):
                 start = (2 * (first + i) + v) * P
-                return words[:, start : start + P]
+                return words[:, r % 2, start : start + P]
 
             return word_block
 
@@ -216,7 +223,7 @@ def tile_gin_pa_t_kernel(tc, X, A, W_in_words, W_in_scales, b_in, eps0, out):
             a_grouped[unit] = transpose_and_group(
                 a_word_block(r, first), n, vector_banks=1 if first == 0 and r < LAST else 0
             )
-            if len(a_rows) < NODE_TILES:
+            if r % 2 == 1 and len(a_rows) < PAIRS:
                 load_a()
 
         def quantise_unit(unit):
@@ -260,7 +267,7 @@ def tile_gin_pa_t_kernel(tc, X, A, W_in_words, W_in_scales, b_in, eps0, out):
                 op1=ADD,
             )
             due = r1 % STORE_TILES == 0 or r1 >= NODE_TILES - 2
-            if due and len(a_rows) == NODE_TILES:
+            if due and len(a_rows) == PAIRS:
                 store(stored_to[0], r1)
                 stored_to[0] = r1
 

from contextlib import ExitStack

import concourse.masks as masks
import concourse.mybir as mybir

F32 = mybir.dt.float32
BF16 = mybir.dt.bfloat16
I32 = mybir.dt.int32
U32 = mybir.dt.uint32
U8 = mybir.dt.uint8
FP8X4 = mybir.dt.float8_e4m3fn_x4
ADD = mybir.AluOpType.add
MULT = mybir.AluOpType.mult

P = 128
PACK = 4
K_PASS = P * PACK
NODES = 4096
IN_DIM = 512
HID = 128
NODE_TILES = NODES // P
PASSES = NODES // K_PASS
PAIRS = NODE_TILES // 2
A_BUFS = 5
WHOLE_PAIRS = 8
STORE_TILES = 4

FLOPS = 2 * NODES * IN_DIM * HID + 2 * NODES * NODES * HID


def tile_gin_pa_t_kernel(tc, X, A, W_in_words, W_in_scales, b_in, eps0, out):
    nc = tc.nc

    x_view = X.rearrange("(g q p e) k -> g p q (e k)", g=PASSES, q=2, p=P, e=2)
    a_view = A.rearrange("(d p e) k -> d p e k", d=PAIRS, p=P, e=2)
    out_view = out.rearrange("(d p e) n -> p d (e n)", d=PAIRS, p=P, e=2)

    with ExitStack() as ctx:
        const = ctx.enter_context(tc.tile_pool(name="const", bufs=1))
        x_pool = ctx.enter_context(tc.tile_pool(name="x_rows", bufs=PASSES))
        a_pool = ctx.enter_context(tc.tile_pool(name="a_rows", bufs=A_BUFS))
        grouped_pool = ctx.enter_context(
            tc.tile_pool(name="grouped", bufs=4)
        )
        mx_pool = ctx.enter_context(tc.tile_pool(name="mx", bufs=6))
        transposed_banks = ctx.enter_context(tc.psum_pool(name="transposed", bufs=6))
        sum_banks = ctx.enter_context(tc.psum_pool(name="sums", bufs=2))
        ctx.enter_context(tc.manual_schedule())

        ident = const.tile([P, P], F32, name="ident")
        masks.make_identity(nc, ident[:])

        x_rows = []

        def load_x(g):
            rows = x_pool.tile([P, PACK, IN_DIM], BF16, name="x_rows")
            nc.sync.dma_start(
                out=rows[:].rearrange("p (q e) k -> p q (e k)", e=2), in_=x_view[g]
            )
            x_rows.append(rows)

        load_x(0)

        bias_row = const.tile([P, HID], BF16, name="bias_row")
        eps_row = const.tile([P, 2], BF16, name="eps_row")
        nc.vector.memset(bias_row[:], 0.0)
        nc.vector.memset(eps_row[:], 0.0)
        nc.sync.dma_start(out=bias_row[0:1, :], in_=b_in.unsqueeze(0))
        w_codes = const.tile([P, HID * PACK], U8, name="w_codes", align_bytes=64)
        nc.sync.dma_start(
            out=w_codes[:].bitcast(I32),
            in_=W_in_words[0].rearrange("p n t -> p (n t)").bitcast(I32),
        )
        load_x(1)
        load_x(2)
        w_scales = const.tile([P, HID], U8, name="w_scales", align_bytes=64)
        nc.vector.memset(w_scales[:].bitcast(I32), 0)
        for quadrant in range(4):
            nc.sync.dma_start(
                out=w_scales[32 * quadrant : 32 * quadrant + 4, :].bitcast(I32),
                in_=W_in_scales[0, 4 * quadrant : 4 * quadrant + 4, :].bitcast(I32),
            )
        for g in range(3, PASSES):
            load_x(g)
        nc.sync.dma_start(out=eps_row[0:1, 0:1], in_=eps0.unsqueeze(0))

        a_rows = []

        LAST = NODE_TILES - 1
        units = [(r, 0, PASSES) for r in range(LAST - 1)]
        next_to_last = [(LAST - 1, 0, 4), (LAST - 1, 4, 4)]
        last = [(LAST, 0, 4), (LAST, 4, 2), (LAST, 6, 2)]

        def load_a():
            d = len(a_rows)
            rows = a_pool.tile([P, 2, NODES], BF16, name="a_rows")
            if d < WHOLE_PAIRS:
                nc.sync.dma_start(
                    out=rows[:].rearrange("p e k -> p (e k)"),
                    in_=a_view[d].rearrange("p e k -> p (e k)"),
                )
            else:
                for r, first, n in units + next_to_last + last:
                    if r // 2 == d:
                        k = slice(first * K_PASS, (first + n) * K_PASS)
                        nc.sync.dma_start(out=rows[:, r % 2, k], in_=a_view[d, :, r % 2, k])
            a_rows.append(rows)

        for d in range(A_BUFS):
            load_a()

        ones = const.tile([P, P], BF16, name="ones")
        nc.vector.memset(ones[:], 1.0)
        bias = const.tile([P, HID], F32, name="bias")
        self_weight = const.tile([P, 1], F32, name="self_weight")

        def spread_bias():
            spread = sum_banks.tile([P, HID], F32, name="bias_sum", tag="sums")
            nc.tensor.matmul(out=spread[:], lhsT=ones[:], rhs=bias_row[:], start=True, stop=True)
            nc.vector.tensor_copy(out=bias[:], in_=spread[:])

        def spread_eps():
            spread = sum_banks.tile([P, 2], F32, name="eps_sum", tag="sums")
            nc.tensor.matmul(out=spread[:], lhsT=ones[:], rhs=eps_row[:], start=True, stop=True)
            nc.vector.tensor_scalar_add(out=self_weight[:], in0=spread[:, 0:1], scalar1=1.0)

        h_f32 = const.tile([P, NODE_TILES, HID], F32, name="h_f32")
        h_grouped = const.tile([P, PASSES, HID, PACK], BF16, name="h_grouped", align_bytes=64)
        h_codes = const.tile([P, PASSES * HID], U32, name="h_codes", align_bytes=64)
        h_scales = const.tile([P, PASSES * HID], U8, name="h_scales", align_bytes=64)

        def transpose_and_group(word_block, operands, vector_banks):
            grouped = grouped_pool.tile(
                [P, operands, P, PACK], BF16, name="grouped", align_bytes=64
            )
            grouped_words = grouped[:].bitcast(F32)
            for b in range(operands // 2):
                bank = transposed_banks.tile([P, 2, 2, P], F32, name="bank")
                for j in range(2):
                    for v in range(2):
                        nc.tensor.transpose(bank[:, j, v, :], word_block(2 * b + j, v), ident[:])
                planes_alternately = bank[:].rearrange("p j v r -> p j r v")
                target = grouped_words[:, 2 * b : 2 * b + 2, :, :]
                if b < vector_banks:
                    nc.vector.tensor_copy(out=target, in_=planes_alternately)
                else:
                    nc.scalar.copy(out=target, in_=planes_alternately)
            return grouped

        def quantise(grouped, operands):
            codes = mx_pool.tile([P, operands * P], U32, name="codes", align_bytes=64)
            scales = mx_pool.tile([P, operands * P], U8, name="scales", align_bytes=64)
            nc.vector.quantize_mx(
                out=codes[:].bitcast(FP8X4),
                scales=scales[:],
                in_=grouped[:].rearrange("p i r t -> p (i r t)"),
            )
            return codes, scales

        def x_word_block(g):
            words = x_rows[g][:].bitcast(F32)
            return lambda t, v: words[:, t, v : IN_DIM // 2 : 2]

        def project(g, codes, scales):
            h_sum = sum_banks.tile([P, PACK, HID], F32, name="h_sum", tag="sums")
            for t in range(PACK):
                cols = slice(t * P, (t + 1) * P)
                nc.tensor.matmul_mx(
                    out=h_sum[:, t, :],
                    lhsT=codes[:, cols].bitcast(FP8X4),
                    lhsT_scale=scales[:, cols],
                    rhs=w_codes[:].bitcast(FP8X4),
                    rhs_scale=w_scales[:],
                    start=True,
                    stop=True,
                )
            h_tiles = h_f32[:, PACK * g : PACK * (g + 1), :]
            nc.vector.tensor_tensor(
                out=h_tiles,
                in0=h_sum[:],
                in1=bias[:].unsqueeze(1).to_broadcast([P, PACK, HID]),
                op=ADD,
            )
            nc.scalar.copy(out=h_grouped[:, g], in_=h_tiles.rearrange("p t n -> p n t"))

        def quantise_h(g):
            cols = slice(g * HID, (g + 1) * HID)
            nc.vector.quantize_mx(
                out=h_codes[:, cols].bitcast(FP8X4),
                scales=h_scales[:, cols],
                in_=h_grouped[:, g].rearrange("p n t -> p (n t)"),
            )

        x_grouped = {}
        x_mx = {}
        for turn in range(PASSES + 3):
            if turn < PASSES:
                x_grouped[turn] = transpose_and_group(x_word_block(turn), PACK, vector_banks=1)
            if 0 <= turn - 1 < PASSES:
                x_mx[turn - 1] = quantise(x_grouped[turn - 1], PACK)
            if turn == 1:
                spread_bias()
            if 0 <= turn - 2 < PASSES:
                project(turn - 2, x_mx[turn - 2][0], x_mx[turn - 2][1])
            if 0 <= turn - 3 < PASSES:
                quantise_h(turn - 3)

        def a_word_block(r, first):
            words = a_rows[r // 2][:].bitcast(F32)
            def word_block(i, v):
                start = (2 * (first + i) + v) * P
                return words[:, r % 2, start : start + P]

            return word_block

        results = const.tile([P, NODE_TILES, HID], F32, name="results")
        out_sums = {}
        a_grouped = {}
        a_mx = {}

        def transpose_unit(unit):
            r, first, n = unit
            a_grouped[unit] = transpose_and_group(
                a_word_block(r, first), n, vector_banks=1 if first == 0 and r < LAST else 0
            )
            if r % 2 == 1 and len(a_rows) < PAIRS:
                load_a()

        def quantise_unit(unit):
            a_mx[unit] = quantise(a_grouped[unit], unit[2])

        def aggregate_unit(unit):
            r, first, n = unit
            codes, scales = a_mx[unit]
            shared = r < NODE_TILES - 2
            if first == 0:
                if not shared:
                    bank = sum_banks.tile([P, 1, HID], F32, name="last_sum", tag="sums")
                    out_sums[r] = (bank, 0)
                elif r % 2 == 0:
                    bank = sum_banks.tile([P, 2, HID], F32, name="out_sum", tag="sums")
                    out_sums[r], out_sums[r + 1] = (bank, 0), (bank, 1)
            bank, slot = out_sums[r]
            for i in range(n):
                c = first + i
                cols = slice(i * P, (i + 1) * P)
                h_cols = slice(c * HID, (c + 1) * HID)
                nc.tensor.matmul_mx(
                    out=bank[:, slot, :],
                    lhsT=codes[:, cols].bitcast(FP8X4),
                    lhsT_scale=scales[:, cols],
                    rhs=h_codes[:, h_cols].bitcast(FP8X4),
                    rhs_scale=h_scales[:, h_cols],
                    start=(c == 0),
                    stop=(c == PASSES - 1),
                )
            if first + n == PASSES and (r % 2 == 1 or not shared):
                finish(r - 1 if shared else r, r + 1, bank)

        def finish(r0, r1, bank):
            nc.vector.scalar_tensor_tensor(
                out=results[:, r0:r1, :],
                in0=h_f32[:, r0:r1, :],
                scalar=self_weight[:, 0:1],
                in1=bank[:],
                op0=MULT,
                op1=ADD,
            )
            due = r1 % STORE_TILES == 0 or r1 >= NODE_TILES - 2
            if due and len(a_rows) == PAIRS:
                store(stored_to[0], r1)
                stored_to[0] = r1

        stored_to = [0]

        def store(r0, r1):
            if r1 - r0 == 1:
                cols = slice(r0 % 2 * HID, (r0 % 2 + 1) * HID)
                nc.sync.dma_start(out=out_view[:, r0 // 2, cols], in_=results[:, r0, :])
            else:
                nc.sync.dma_start(
                    out=out_view[:, r0 // 2 : r1 // 2, :],
                    in_=results[:, r0:r1, :].rearrange("p (d e) n -> p d (e n)", e=2),
                )

        spread_eps()
        for turn, unit in enumerate(units):
            transpose_unit(unit)
            if turn >= 1:
                quantise_unit(units[turn - 1])
            if turn >= 2:
                aggregate_unit(units[turn - 2])
        for unit in next_to_last:
            transpose_unit(unit)
        quantise_unit(units[-1])
        aggregate_unit(units[-2])
        for unit in last[:-1]:
            transpose_unit(unit)
        for unit in next_to_last:
            quantise_unit(unit)
        transpose_unit(last[-1])
        quantise_unit(last[0])
        aggregate_unit(units[-1])
        for unit in last[1:]:
            quantise_unit(unit)
        for unit in next_to_last + last:
            aggregate_unit(unit)
